import numpy as np
import ml_dtypes


def mxq(x, axis, fmt="e4m3"):
    dtype, down = {"e4m3": (ml_dtypes.float8_e4m3fn, 7), "e5m2": (ml_dtypes.float8_e5m2, 14)}[fmt]
    v = np.moveaxis(np.asarray(x, np.float32).astype(ml_dtypes.bfloat16).astype(np.float64), axis, -1)
    blocks = v.reshape(v.shape[:-1] + (-1, 32))
    amax = np.abs(blocks).max(-1, keepdims=True)
    byte = np.maximum(np.where(amax > 0, np.frexp(amax)[1] - 1 + 127, 0) - down, 1)
    scale = np.exp2(byte - 127.0)
    codes = (blocks / scale).astype(np.float32).astype(dtype).astype(np.float64)
    return np.moveaxis((codes * scale).reshape(v.shape), -1, axis)


WIDE = False


def mx_kscale(k):
    if not WIDE:
        return np.ones(k)
    levels = np.array([10, -10, 5, -5, 0])
    a = np.random.permutation(np.resize(levels, k // 512 * 4)).reshape(k // 512, 4)
    idx = np.arange(k)
    return np.exp2(a[idx // 512, idx % 128 // 32])


BF16 = ml_dtypes.bfloat16


def bf(x):
    return np.asarray(x, np.float32).astype(BF16)


def f64(x):
    return np.asarray(x).astype(np.float64)


E2M1 = np.array([0.0, 0.5, 1.0, 1.5, 2.0, 3.0, 4.0, 6.0, -0.0, -0.5, -1.0, -1.5, -2.0, -3.0, -4.0, -6.0])


def pack_weight(w, fmt):
    k, n = w.shape
    w = f64(bf(w)).reshape(k // 32, 32, n)
    amax = np.abs(w).max(1)
    if fmt == "e4m3":
        byte = np.frexp(amax)[1] - 1 + 127 - 7
    else:
        mant, ex = np.frexp(amax / 6.0)
        byte = np.where(mant > 0.5, ex, ex - 1) + 127
    byte = np.clip(np.where(amax > 0, byte, 1), 1, 254)
    scaled = (w * np.exp2(127.0 - byte)[:, None, :]).reshape(k, n).astype(np.float32)
    by_word = np.ascontiguousarray(scaled.reshape(k // 512, 128, 4, n).transpose(0, 1, 3, 2))
    if fmt == "e4m3":
        words = by_word.astype(ml_dtypes.float8_e4m3fn).view(np.uint8)
    else:
        c = by_word.astype(ml_dtypes.float4_e2m1fn).view(np.uint8) & 0xF
        words = c[..., 0::2] | (c[..., 1::2] << 4)
    return np.ascontiguousarray(words), np.ascontiguousarray(byte.astype(np.uint8).reshape(k // 512, 16, n))


def unpack_weight(words, scales, fmt):
    g, p, n, _ = words.shape
    if fmt == "e4m3":
        vals = np.ascontiguousarray(words).view(ml_dtypes.float8_e4m3fn).astype(np.float64)
    else:
        nib = np.empty((g, p, n, 4), np.uint8)
        nib[..., 0::2] = words & 0xF
        nib[..., 1::2] = words >> 4
        vals = E2M1[nib]
    vals = vals * np.repeat(np.exp2(scales.astype(np.float64) - 127.0), 8, axis=1)[..., None]
    return vals.transpose(0, 1, 3, 2).reshape(g * 512, n)


B, S, I, O = 8, 16, 4096, 4096


def setup_inputs():
    s = mx_kscale(I)
    hidden_states = bf(np.random.standard_normal((B, S, I)) * s)
    w = np.random.standard_normal((I, O)) / 64.0 / s[:, None]
    weight_words, weight_scales = pack_weight(w, "e4m3")
    return {"hidden_states": hidden_states, "weight_words": weight_words, "weight_scales": weight_scales}


def reference(hidden_states, weight_words, weight_scales):
    w = unpack_weight(weight_words, weight_scales, "e4m3")
    return mxq(f64(hidden_states), 2, "e4m3") @ w

@@ -1,0 +1,117 @@
+from contextlib import ExitStack
+
+import concourse.mybir as mybir
+from concourse.masks import make_identity
+
+FP8X4 = mybir.dt.float8_e4m3fn_x4
+BF16 = mybir.dt.bfloat16
+F32 = mybir.dt.float32
+I32 = mybir.dt.int32
+U32 = mybir.dt.uint32
+U8 = mybir.dt.uint8
+
+P = 128
+K = 4096
+N = 4096
+GROUPS = K // 512
+N_TILE = 512
+BANKS = N // N_TILE
+
+FLOPS = 2 * P * K * N
+
+
+def weight_chunks():
+    chunks = [(g, 0, N) for g in range(GROUPS - 2)]
+    for c in range(0, N - 1024, 1024):
+        chunks.append((GROUPS - 2, c, c + 1024))
+        chunks.append((GROUPS - 1, c, c + 1024))
+    chunks.append((GROUPS - 2, N - 1024, N))
+    chunks.append((GROUPS - 1, N - 1024, N - 512))
+    chunks.append((GROUPS - 1, N - 512, N))
+    return chunks
+
+
+def tile_nvfp4linear_kernel(tc, hidden_states, weight_words, weight_scales, out):
+    nc = tc.nc
+    x_dram = hidden_states.rearrange("b s k -> (b s) k")
+    out_dram = out.rearrange("b s n -> (b s) n")
+
+    with ExitStack() as ctx:
+        keep = ctx.enter_context(tc.tile_pool(name="keep", bufs=1))
+        psum = ctx.enter_context(tc.psum_pool(name="psum", bufs=1))
+        ctx.enter_context(tc.manual_schedule())
+
+        x_sb = keep.tile([P, K], BF16, name="x_sb", align_bytes=64)
+        ident = keep.tile([P, P], F32, name="ident")
+        grouped = keep.tile([P, GROUPS, P, 4], BF16, name="grouped", align_bytes=64)
+        x_codes = keep.tile([P, GROUPS * P], U32, name="x_codes", align_bytes=64)
+        x_scales = keep.tile([P, GROUPS * P], U8, name="x_scales", align_bytes=64)
+        planes = [keep.tile([P, N], U8, name="planes%d" % h, align_bytes=64) for h in range(2)]
+        w = [keep.tile([P, 4 * N], U8, name="w%d" % g, align_bytes=64) for g in range(GROUPS)]
+        res = [keep.tile([P, 2 * N_TILE], F32, name="res%d" % i) for i in range(BANKS // 2)]
+
+        for h in range(2):
+            nc.vector.memset(planes[h][:].bitcast(I32), 0)
+        make_identity(nc, ident[:])
+
+        nc.sync.dma_start(out=x_sb[:], in_=x_dram)
+        for h in range(2):
+            for q in range(4):
+                nc.sync.dma_start(
+                    out=planes[h][32 * q : 32 * q + 16, :].bitcast(I32),
+                    in_=weight_scales[4 * h : 4 * h + 4, 4 * q : 4 * q + 4, :].bitcast(I32),
+                )
+        chunks = weight_chunks()
+        for g, c0, c1 in chunks:
+            nc.sync.dma_start(
+                out=w[g][:, 4 * c0 : 4 * c1].bitcast(I32),
+                in_=weight_words[g].rearrange("p n t -> p (n t)")[:, 4 * c0 : 4 * c1].bitcast(I32),
+            )
+
+        x_words = x_sb[:].bitcast(F32)
+        grouped_words = grouped[:].bitcast(F32)
+        xt = []
+        for i in range(GROUPS // 2):
+            xt_i = psum.tile([P, 4, P], F32, name="xt%d" % i, tag="bank%d" % i)
+            xt.append(xt_i)
+            for s in range(4):
+                g, u = 2 * i + s // 2, s % 2
+                nc.tensor.transpose(xt_i[:, s, :], x_words[:, 256 * g + u : 256 * (g + 1) : 2], ident[:])
+        for i in range(GROUPS // 2):
+            src = xt[i][:].rearrange("p (g u) m -> p g m u", u=2)
+            dst = grouped_words[:, 2 * i : 2 * i + 2, :, :]
+            if i % 2 == 0:
+                nc.vector.tensor_copy(out=dst, in_=src)
+            else:
+                nc.scalar.copy(out=dst, in_=src)
+        for c in range(2):
+            nc.vector.quantize_mx(
+                out=x_codes[:, 512 * c : 512 * (c + 1)].bitcast(FP8X4),
+                scales=x_scales[:, 512 * c : 512 * (c + 1)],
+                in_=grouped[:, 4 * c : 4 * c + 4, :, :].rearrange("p g m t -> p (g m t)"),
+            )
+
+        acc = [psum.tile([P, N_TILE], F32, name="acc%d" % b, tag="bank%d" % b) for b in range(BANKS)]
+        for g, c0, c1 in chunks:
+            k_off = 4 * (g % 4)
+            for b in range(c0 // N_TILE, c1 // N_TILE):
+                nc.tensor.matmul_mx(
+                    out=acc[b][:],
+                    lhsT=x_codes[:, P * g : P * (g + 1)].bitcast(FP8X4),
+                    lhsT_scale=x_scales[:, P * g : P * (g + 1)],
+                    rhs=w[g][:, 4 * N_TILE * b : 4 * N_TILE * (b + 1)].bitcast(FP8X4),
+                    rhs_scale=planes[g // 4][k_off:P, N_TILE * b : N_TILE * (b + 1)],
+                    start=(g == 0),
+                    stop=(g == GROUPS - 1),
+                )
+            if g == GROUPS - 1:
+                for b in range(c0 // N_TILE, c1 // N_TILE):
+                    dst = res[b // 2][:, N_TILE * (b % 2) : N_TILE * (b % 2 + 1)]
+                    if b % 2 == 0:
+                        nc.vector.tensor_copy(out=dst, in_=acc[b][:])
+                    else:
+                        nc.scalar.copy(out=dst, in_=acc[b][:])
+                nc.sync.dma_start(
+                    out=out_dram[:, c0:c1],
+                    in_=res[c0 // (2 * N_TILE)][:, c0 % (2 * N_TILE) : c0 % (2 * N_TILE) + c1 - c0],
+                )

@@ -57,9 +57,9 @@ def tile_nvfp4linear_kernel(tc, hidden_states, weight_words, weight_scales, out)
         nc.sync.dma_start(out=x_sb[:], in_=x_dram)
         for h in range(2):
             for q in range(4):
-                nc.sync.dma_start(
-                    out=planes[h][32 * q : 32 * q + 16, :].bitcast(I32),
-                    in_=weight_scales[4 * h : 4 * h + 4, 4 * q : 4 * q + 4, :].bitcast(I32),
+                nc.gpsimd.dma_start(
+                    out=planes[h][32 * q : 32 * q + 16, :].bitcast(F32),
+                    in_=weight_scales[4 * h : 4 * h + 4, 4 * q : 4 * q + 4, :].bitcast(F32),
                 )
         chunks = weight_chunks()
         for g, c0, c1 in chunks:

@@ -46,20 +46,20 @@ def tile_nvfp4linear_kernel(tc, hidden_states, weight_words, weight_scales, out)
         grouped = keep.tile([P, GROUPS, P, 4], BF16, name="grouped", align_bytes=64)
         x_codes = keep.tile([P, GROUPS * P], U32, name="x_codes", align_bytes=64)
         x_scales = keep.tile([P, GROUPS * P], U8, name="x_scales", align_bytes=64)
-        planes = [keep.tile([P, N], U8, name="planes%d" % h, align_bytes=64) for h in range(2)]
+        planes = keep.tile([P, 2, N], U8, name="planes", align_bytes=64)
         w = [keep.tile([P, 4 * N], U8, name="w%d" % g, align_bytes=64) for g in range(GROUPS)]
         res = [keep.tile([P, 2 * N_TILE], F32, name="res%d" % i) for i in range(BANKS // 2)]
 
-        for h in range(2):
-            nc.vector.memset(planes[h][:].bitcast(I32), 0)
+        nc.vector.memset(planes[:].rearrange("p h n -> p (h n)").bitcast(I32), 0)
         make_identity(nc, ident[:])
 
         nc.sync.dma_start(out=x_sb[:], in_=x_dram)
-        for h in range(2):
+        scale_rows = weight_scales.rearrange("(h j) q n -> j h q n", h=2)
+        for r in range(4):
             for q in range(4):
                 nc.gpsimd.dma_start(
-                    out=planes[h][32 * q : 32 * q + 16, :].bitcast(F32),
-                    in_=weight_scales[4 * h : 4 * h + 4, 4 * q : 4 * q + 4, :].bitcast(F32),
+                    out=planes[32 * q + r : 32 * q + 16 : 4, :, :].bitcast(F32),
+                    in_=scale_rows[:, :, 4 * q + r, :].bitcast(F32),
                 )
         chunks = weight_chunks()
         for g, c0, c1 in chunks:
@@ -100,7 +100,7 @@ def tile_nvfp4linear_kernel(tc, hidden_states, weight_words, weight_scales, out)
                     lhsT=x_codes[:, P * g : P * (g + 1)].bitcast(FP8X4),
                     lhsT_scale=x_scales[:, P * g : P * (g + 1)],
                     rhs=w[g][:, 4 * N_TILE * b : 4 * N_TILE * (b + 1)].bitcast(FP8X4),
-                    rhs_scale=planes[g // 4][k_off:P, N_TILE * b : N_TILE * (b + 1)],
+                    rhs_scale=planes[k_off:P, g // 4, N_TILE * b : N_TILE * (b + 1)],
                     start=(g == 0),
                     stop=(g == GROUPS - 1),
                 )

@@ -54,9 +54,15 @@ def tile_nvfp4linear_kernel(tc, hidden_states, weight_words, weight_scales, out)
         make_identity(nc, ident[:])
 
         nc.sync.dma_start(out=x_sb[:], in_=x_dram)
+        for h in range(2):
+            for q in range(2):
+                nc.sync.dma_start(
+                    out=planes[32 * q : 32 * q + 16, h, :].bitcast(I32),
+                    in_=weight_scales[4 * h : 4 * h + 4, 4 * q : 4 * q + 4, :].bitcast(I32),
+                )
         scale_rows = weight_scales.rearrange("(h j) q n -> j h q n", h=2)
         for r in range(4):
-            for q in range(4):
+            for q in range(2, 4):
                 nc.gpsimd.dma_start(
                     out=planes[32 * q + r : 32 * q + 16 : 4, :, :].bitcast(F32),
                     in_=scale_rows[:, :, 4 * q + r, :].bitcast(F32),

from contextlib import ExitStack

import concourse.mybir as mybir
from concourse.masks import make_identity

FP8X4 = mybir.dt.float8_e4m3fn_x4
BF16 = mybir.dt.bfloat16
F32 = mybir.dt.float32
I32 = mybir.dt.int32
U32 = mybir.dt.uint32
U8 = mybir.dt.uint8

P = 128
K = 4096
N = 4096
GROUPS = K // 512
N_TILE = 512
BANKS = N // N_TILE

FLOPS = 2 * P * K * N


def weight_chunks():
    chunks = [(g, 0, N) for g in range(GROUPS - 2)]
    for c in range(0, N - 1024, 1024):
        chunks.append((GROUPS - 2, c, c + 1024))
        chunks.append((GROUPS - 1, c, c + 1024))
    chunks.append((GROUPS - 2, N - 1024, N))
    chunks.append((GROUPS - 1, N - 1024, N - 512))
    chunks.append((GROUPS - 1, N - 512, N))
    return chunks


def tile_nvfp4linear_kernel(tc, hidden_states, weight_words, weight_scales, out):
    nc = tc.nc
    x_dram = hidden_states.rearrange("b s k -> (b s) k")
    out_dram = out.rearrange("b s n -> (b s) n")

    with ExitStack() as ctx:
        keep = ctx.enter_context(tc.tile_pool(name="keep", bufs=1))
        psum = ctx.enter_context(tc.psum_pool(name="psum", bufs=1))
        ctx.enter_context(tc.manual_schedule())

        x_sb = keep.tile([P, K], BF16, name="x_sb", align_bytes=64)
        ident = keep.tile([P, P], F32, name="ident")
        grouped = keep.tile([P, GROUPS, P, 4], BF16, name="grouped", align_bytes=64)
        x_codes = keep.tile([P, GROUPS * P], U32, name="x_codes", align_bytes=64)
        x_scales = keep.tile([P, GROUPS * P], U8, name="x_scales", align_bytes=64)
        planes = keep.tile([P, 2, N], U8, name="planes", align_bytes=64)
        w = [keep.tile([P, 4 * N], U8, name="w%d" % g, align_bytes=64) for g in range(GROUPS)]
        res = [keep.tile([P, 2 * N_TILE], F32, name="res%d" % i) for i in range(BANKS // 2)]

        nc.vector.memset(planes[:].rearrange("p h n -> p (h n)").bitcast(I32), 0)
        make_identity(nc, ident[:])

        nc.sync.dma_start(out=x_sb[:], in_=x_dram)
        for h in range(2):
            for q in range(2):
                nc.sync.dma_start(
                    out=planes[32 * q : 32 * q + 16, h, :].bitcast(I32),
                    in_=weight_scales[4 * h : 4 * h + 4, 4 * q : 4 * q + 4, :].bitcast(I32),
                )
        scale_rows = weight_scales.rearrange("(h j) q n -> j h q n", h=2)
        for r in range(4):
            for q in range(2, 4):
                nc.gpsimd.dma_start(
                    out=planes[32 * q + r : 32 * q + 16 : 4, :, :].bitcast(F32),
                    in_=scale_rows[:, :, 4 * q + r, :].bitcast(F32),
                )
        chunks = weight_chunks()
        for g, c0, c1 in chunks:
            nc.sync.dma_start(
                out=w[g][:, 4 * c0 : 4 * c1].bitcast(I32),
                in_=weight_words[g].rearrange("p n t -> p (n t)")[:, 4 * c0 : 4 * c1].bitcast(I32),
            )

        x_words = x_sb[:].bitcast(F32)
        grouped_words = grouped[:].bitcast(F32)
        xt = []
        for i in range(GROUPS // 2):
            xt_i = psum.tile([P, 4, P], F32, name="xt%d" % i, tag="bank%d" % i)
            xt.append(xt_i)
            for s in range(4):
                g, u = 2 * i + s // 2, s % 2
                nc.tensor.transpose(xt_i[:, s, :], x_words[:, 256 * g + u : 256 * (g + 1) : 2], ident[:])
        for i in range(GROUPS // 2):
            src = xt[i][:].rearrange("p (g u) m -> p g m u", u=2)
            dst = grouped_words[:, 2 * i : 2 * i + 2, :, :]
            if i % 2 == 0:
                nc.vector.tensor_copy(out=dst, in_=src)
            else:
                nc.scalar.copy(out=dst, in_=src)
        for c in range(2):
            nc.vector.quantize_mx(
                out=x_codes[:, 512 * c : 512 * (c + 1)].bitcast(FP8X4),
                scales=x_scales[:, 512 * c : 512 * (c + 1)],
                in_=grouped[:, 4 * c : 4 * c + 4, :, :].rearrange("p g m t -> p (g m t)"),
            )

        acc = [psum.tile([P, N_TILE], F32, name="acc%d" % b, tag="bank%d" % b) for b in range(BANKS)]
        for g, c0, c1 in chunks:
            k_off = 4 * (g % 4)
            for b in range(c0 // N_TILE, c1 // N_TILE):
                nc.tensor.matmul_mx(
                    out=acc[b][:],
                    lhsT=x_codes[:, P * g : P * (g + 1)].bitcast(FP8X4),
                    lhsT_scale=x_scales[:, P * g : P * (g + 1)],
                    rhs=w[g][:, 4 * N_TILE * b : 4 * N_TILE * (b + 1)].bitcast(FP8X4),
                    rhs_scale=planes[k_off:P, g // 4, N_TILE * b : N_TILE * (b + 1)],
                    start=(g == 0),
                    stop=(g == GROUPS - 1),
                )
            if g == GROUPS - 1:
                for b in range(c0 // N_TILE, c1 // N_TILE):
                    dst = res[b // 2][:, N_TILE * (b % 2) : N_TILE * (b % 2 + 1)]
                    if b % 2 == 0:
                        nc.vector.tensor_copy(out=dst, in_=acc[b][:])
                    else:
                        nc.scalar.copy(out=dst, in_=acc[b][:])
                nc.sync.dma_start(
                    out=out_dram[:, c0:c1],
                    in_=res[c0 // (2 * N_TILE)][:, c0 % (2 * N_TILE) : c0 % (2 * N_TILE) + c1 - c0],
                )
